import numpy as np
import ml_dtypes


def mxq(x, axis, fmt="e4m3"):
    dtype, down = {"e4m3": (ml_dtypes.float8_e4m3fn, 7), "e5m2": (ml_dtypes.float8_e5m2, 14)}[fmt]
    v = np.moveaxis(np.asarray(x, np.float32).astype(ml_dtypes.bfloat16).astype(np.float64), axis, -1)
    blocks = v.reshape(v.shape[:-1] + (-1, 32))
    amax = np.abs(blocks).max(-1, keepdims=True)
    byte = np.maximum(np.where(amax > 0, np.frexp(amax)[1] - 1 + 127, 0) - down, 1)
    scale = np.exp2(byte - 127.0)
    codes = (blocks / scale).astype(np.float32).astype(dtype).astype(np.float64)
    return np.moveaxis((codes * scale).reshape(v.shape), -1, axis)


WIDE = False


def mx_kscale(k):
    if not WIDE:
        return np.ones(k)
    levels = np.array([10, -10, 5, -5, 0])
    a = np.random.permutation(np.resize(levels, k // 512 * 4)).reshape(k // 512, 4)
    idx = np.arange(k)
    return np.exp2(a[idx // 512, idx % 128 // 32])


BF16 = ml_dtypes.bfloat16


def bf(x):
    return np.asarray(x, np.float32).astype(BF16)


def f64(x):
    return np.asarray(x).astype(np.float64)


B, N, DIM, QK, HID = 4, 2048, 1024, 128, 64
EPS = 1e-5
C_SIM = 6.0


def silu(v):
    return v / (1.0 + np.exp(-v))


def setup_inputs():
    s = mx_kscale(DIM)
    r = 10.0 ** np.random.uniform(-2.5, 0.5, (B, N, 1))
    sq = np.sqrt(C_SIM * np.sqrt(N) / np.sqrt(QK))
    return {"x": bf(np.random.standard_normal((B, N, DIM)) * r),
            "ln_scale": bf((1.0 + 0.1 * np.random.standard_normal(DIM)) * s),
            "ln_bias": bf(0.2 * np.random.standard_normal(DIM) * s),
            "W_hidden": bf(np.random.standard_normal((DIM, 2 * HID)) / np.sqrt(DIM) / s[:, None]),
            "b_hidden": bf(0.3 * np.random.standard_normal(2 * HID)),
            "W_qk": bf(np.random.standard_normal((DIM, QK)) / np.sqrt(DIM) / s[:, None]),
            "b_qk": bf(0.3 * np.random.standard_normal(QK)),
            "os_weight": bf(np.random.standard_normal((2, QK)) * sq / 0.6),
            "os_bias": bf(np.random.standard_normal((2, QK)))}


def reference(x, ln_scale, ln_bias, W_hidden, b_hidden, W_qk, b_qk, os_weight, os_bias):
    x = f64(x)
    mu = x.mean(-1, keepdims=True)
    var = np.square(x - mu).mean(-1, keepdims=True)
    xn = (x - mu) / np.sqrt(var + EPS) * f64(ln_scale) + f64(ln_bias)
    xq = mxq(xn, 2, "e4m3")
    hid = silu((xq @ mxq(f64(W_hidden), 0, "e4m3")) + f64(b_hidden))
    v, gate = hid[..., :HID], hid[..., HID:]
    qk = silu((xq @ mxq(f64(W_qk), 0, "e4m3")) + f64(b_qk))
    qk2 = qk[..., None, :] * f64(os_weight) + f64(os_bias)
    return v, gate, qk2[..., 0, :], qk2[..., 1, :]

@@ -1,0 +1,219 @@
+import concourse.mybir as mybir
+from concourse.masks import make_identity
+
+F32 = mybir.dt.float32
+BF16 = mybir.dt.bfloat16
+U32 = mybir.dt.uint32
+U8 = mybir.dt.uint8
+FP8X4 = mybir.dt.float8_e4m3fn_x4
+ALU = mybir.AluOpType
+ACT = mybir.ActivationFunctionType
+
+P = 128
+DIM = 1024
+TOKENS = 8192
+SUB = 4
+BLOCK = P * SUB
+NB = TOKENS // BLOCK
+CHUNKS = DIM // P
+PACK = 4
+PASSES = 2
+EPS = 1e-5
+FLOPS = 2 * TOKENS * DIM * 256
+
+P2_ENGINE = ("v", "s", "v", "s")
+EXIT_ENGINE = ("s", "s", "s", "s", "s", "s", "s", "s")
+OUT_ENGINE = ("s", "s", "s")
+
+
+def tile_gau_pa_t_kernel(
+    tc, x, ln_scale, ln_bias, W_hidden, b_hidden, W_qk, b_qk, os_weight, os_bias, out_0, out_1, out_2, out_3
+):
+    nc = tc.nc
+    xv = x.flatten_outer_dims().rearrange("(b p s) k -> b p s k", p=P, s=SUB)
+    vv = out_0.flatten_outer_dims().rearrange("(b p s) d -> b p s d", p=P, s=SUB)
+    gv = out_1.flatten_outer_dims().rearrange("(b p s) d -> b p s d", p=P, s=SUB)
+    qv = out_2.flatten_outer_dims().rearrange("(b p s) d -> b p s d", p=P, s=SUB)
+    kv = out_3.flatten_outer_dims().rearrange("(b p s) d -> b p s d", p=P, s=SUB)
+
+    with tc.tile_pool(name="const", bufs=1) as const, tc.tile_pool(name="xin", bufs=4) as xin, tc.tile_pool(
+        name="stat", bufs=4
+    ) as stat, tc.tile_pool(name="ynorm", bufs=8) as ynorm, tc.tile_pool(name="mid", bufs=2) as mid, tc.tile_pool(
+        name="quant", bufs=4
+    ) as quant, tc.tile_pool(name="post", bufs=2) as post, tc.tile_pool(name="outs", bufs=3) as outs, tc.psum_pool(
+        name="pyt", bufs=4
+    ) as pyt, tc.psum_pool(name="pacc", bufs=2) as pacc, tc.psum_pool(name="pot", bufs=2) as pot:
+        ident = const.tile([P, P], F32)
+        make_identity(nc, ident[:])
+        neghalf = const.tile([P, SUB], F32)
+        nc.gpsimd.memset(neghalf[:], -0.5)
+
+        rows = const.tile([P, P], BF16)
+        nc.vector.memset(rows[:], 0.0)
+        nc.scalar.dma_start(out=rows[0:8, :], in_=ln_scale.rearrange("(c p) -> c p", p=P))
+        nc.scalar.dma_start(out=rows[8:16, :], in_=ln_bias.rearrange("(c p) -> c p", p=P))
+        nc.scalar.dma_start(out=rows[16:17, :], in_=b_hidden.rearrange("(c p) -> c p", p=P))
+        nc.scalar.dma_start(out=rows[17:18, :], in_=b_qk.rearrange("(c p) -> c p", p=P))
+        nc.scalar.dma_start(out=rows[18:20, :], in_=os_weight)
+        nc.scalar.dma_start(out=rows[20:22, :], in_=os_bias)
+        wraw = const.tile([P, 2, PASSES * PACK, P], BF16)
+        nc.scalar.dma_start(out=wraw[:, 0], in_=W_hidden.rearrange("(c p) n -> p c n", p=P))
+        nc.scalar.dma_start(out=wraw[:, 1], in_=W_qk.rearrange("(c p) n -> p c n", p=P))
+
+        rows32 = const.tile([P, P], F32)
+        nc.vector.tensor_copy(out=rows32[:], in_=rows[:])
+        colps = pot.tile([P, BLOCK], F32, tag="ot")
+        nc.tensor.transpose(out=colps[:, 0:P], in_=rows32[:], identity=ident[:])
+        cols = const.tile([P, 32], F32)
+        nc.vector.tensor_copy(out=cols[:], in_=colps[:, 0:32])
+
+        wgrp = const.tile([P, 2, PASSES, P, PACK], BF16, align_bytes=64)
+        for w in range(2):
+            nc.vector.tensor_copy(
+                out=wgrp[:, w],
+                in_=wraw[:, w].rearrange("p (g j) n -> p g n j", j=PACK),
+            )
+        wcodes = const.tile([P, 2 * PASSES * P], U32, align_bytes=64)
+        wscale = const.tile([P, 2 * PASSES * P], U8, align_bytes=64)
+        nc.vector.quantize_mx(
+            out=wcodes[:].bitcast(FP8X4),
+            scales=wscale[:],
+            in_=wgrp[:].rearrange("p w g n j -> p (w g n j)"),
+        )
+
+        state = {}
+
+        def stage_stats(b):
+            xb = xin.tile([P, SUB, DIM], BF16, tag="xb")
+            nc.sync.dma_start(out=xb[:], in_=xv[b])
+            st = stat.tile([P, SUB, 2, 6], F32, tag="st")
+            mv = stat.tile([P, SUB, 2], F32, tag="mv")
+            for s in range(SUB):
+                for h in range(2):
+                    nc.vector.bn_stats(out=st[:, s, h, :], in_=xb[:, s, 512 * h : 512 * h + 512])
+                nc.vector.bn_aggr(out=mv[:, s, :], in_=st[:, s].rearrange("p h d -> p (h d)"))
+            ve = stat.tile([P, SUB], F32, tag="ve")
+            nc.gpsimd.tensor_scalar(out=ve[:], in0=mv[:, :, 1], scalar1=EPS, scalar2=1.0, op0=ALU.add, op1=ALU.mult)
+            rstd = stat.tile([P, SUB], F32, tag="rstd")
+            nc.gpsimd.tensor_tensor(out=rstd[:], in0=ve[:], in1=neghalf[:], op=ALU.pow)
+            negmu = stat.tile([P, SUB], F32, tag="negmu")
+            nc.gpsimd.tensor_scalar(
+                out=negmu[:], in0=mv[:, :, 0], scalar1=-1.0, scalar2=0.0, op0=ALU.mult, op1=ALU.add
+            )
+            nmr = stat.tile([P, SUB], F32, tag="nmr")
+            nc.gpsimd.tensor_tensor(out=nmr[:], in0=negmu[:], in1=rstd[:], op=ALU.mult)
+            state[b] = {"xb": xb, "mv": mv, "rstd": rstd, "nmr": nmr}
+
+        def stage_main(b):
+            sb = state[b]
+            xb, mv, rstd, nmr = sb["xb"], sb["mv"], sb["rstd"], sb["nmr"]
+            ys = []
+            for s in range(SUB):
+                y = ynorm.tile([P, DIM], F32, tag="y")
+                eng = P2_ENGINE[s]
+                if eng == "v":
+                    nc.vector.tensor_scalar(
+                        out=y[:], in0=xb[:, s, :], scalar1=mv[:, s, 0:1], scalar2=rstd[:, s : s + 1],
+                        op0=ALU.subtract, op1=ALU.mult,
+                    )
+                elif eng == "s":
+                    nc.scalar.activation(
+                        out=y[:], in_=xb[:, s, :], func=ACT.Identity, scale=rstd[:, s : s + 1], bias=nmr[:, s : s + 1]
+                    )
+                else:
+                    nc.gpsimd.tensor_scalar(
+                        out=y[:], in0=xb[:, s, :], scalar1=rstd[:, s : s + 1], scalar2=nmr[:, s : s + 1],
+                        op0=ALU.mult, op1=ALU.add,
+                    )
+                ys.append(y)
+            planes = mid.tile([P, CHUNKS, BLOCK], BF16, tag="planes")
+            codes = []
+            for g in range(PASSES):
+                for j in range(PACK):
+                    c = PACK * g + j
+                    yt = pyt.tile([P, BLOCK], F32, tag="yt")
+                    for s in range(SUB):
+                        nc.tensor.transpose(
+                            out=yt[:, P * s : P * s + P], in_=ys[s][:, P * c : P * c + P], identity=ident[:]
+                        )
+                    if EXIT_ENGINE[c] == "s":
+                        nc.scalar.activation(
+                            out=planes[:, c, :], in_=yt[:], func=ACT.Identity,
+                            scale=cols[:, c : c + 1], bias=cols[:, 8 + c : 9 + c],
+                        )
+                    else:
+                        nc.vector.tensor_scalar(
+                            out=planes[:, c, :], in0=yt[:], scalar1=cols[:, c : c + 1], scalar2=cols[:, 8 + c : 9 + c],
+                            op0=ALU.mult, op1=ALU.add,
+                        )
+                grp = quant.tile([P, BLOCK * PACK], BF16, tag="grp", align_bytes=64)
+                nc.vector.tensor_copy(
+                    out=grp[:].rearrange("p (c i t) -> p c t i", i=4, t=PACK),
+                    in_=planes[:, PACK * g : PACK * g + PACK, :].rearrange("p t (c i) -> p c t i", i=4),
+                )
+                cd = quant.tile([P, BLOCK], U32, tag="cd", align_bytes=64)
+                sc = quant.tile([P, BLOCK], U8, tag="sc", align_bytes=64)
+                nc.vector.quantize_mx(out=cd[:].bitcast(FP8X4), scales=sc[:], in_=grp[:])
+                codes.append((cd, sc))
+            sb["codes"] = codes
+
+        def stage_post(b):
+            codes = state[b]["codes"]
+            accs = []
+            for w in range(2):
+                acc = pacc.tile([P, BLOCK], F32, tag="acc")
+                for g in range(PASSES):
+                    o = (w * PASSES + g) * P
+                    nc.tensor.matmul_mx(
+                        out=acc[:],
+                        lhsT=wcodes[:, o : o + P].bitcast(FP8X4),
+                        lhsT_scale=wscale[:, o : o + P],
+                        rhs=codes[g][0][:].bitcast(FP8X4),
+                        rhs_scale=codes[g][1][:],
+                        start=(g == 0),
+                        stop=(g == PASSES - 1),
+                    )
+                accs.append(acc)
+            hidT = post.tile([P, BLOCK], F32, tag="hidT")
+            nc.scalar.activation(out=hidT[:], in_=accs[0][:], func=ACT.Silu, bias=cols[:, 16:17], scale=1.0)
+            qkT = post.tile([P, BLOCK], F32, tag="qkT")
+            nc.scalar.activation(out=qkT[:], in_=accs[1][:], func=ACT.Silu, bias=cols[:, 17:18], scale=1.0)
+            qT = post.tile([P, BLOCK], F32, tag="qT")
+            nc.vector.tensor_scalar(
+                out=qT[:], in0=qkT[:], scalar1=cols[:, 18:19], scalar2=cols[:, 20:21], op0=ALU.mult, op1=ALU.add
+            )
+            kT = post.tile([P, BLOCK], F32, tag="kT")
+            nc.vector.tensor_scalar(
+                out=kT[:], in0=qkT[:], scalar1=cols[:, 19:20], scalar2=cols[:, 21:22], op0=ALU.mult, op1=ALU.add
+            )
+            for i, src in enumerate((hidT, qT, kT)):
+                ot = pot.tile([P, BLOCK], F32, tag="ot")
+                for s in range(SUB):
+                    nc.tensor.transpose(out=ot[:, P * s : P * s + P], in_=src[:, P * s : P * s + P], identity=ident[:])
+                res = outs.tile([P, BLOCK], F32, tag="res%d" % i)
+                if i == 0:
+                    dst = res[:].rearrange("p (h s d) -> p s h d", h=2, s=SUB)
+                    srcv = ot[:].rearrange("p (s h d) -> p s h d", s=SUB, h=2)
+                else:
+                    dst = res[:]
+                    srcv = ot[:]
+                if OUT_ENGINE[i] == "s":
+                    nc.scalar.copy(out=dst, in_=srcv)
+                else:
+                    nc.vector.tensor_copy(out=dst, in_=srcv)
+                if i == 0:
+                    halves = res[:].rearrange("p (h s d) -> p h s d", h=2, s=SUB)
+                    nc.sync.dma_start(out=vv[b], in_=halves[:, 0])
+                    nc.sync.dma_start(out=gv[b], in_=halves[:, 1])
+                elif i == 1:
+                    nc.sync.dma_start(out=qv[b], in_=res[:].rearrange("p (s d) -> p s d", s=SUB))
+                else:
+                    nc.sync.dma_start(out=kv[b], in_=res[:].rearrange("p (s d) -> p s d", s=SUB))
+
+        for it in range(NB + 2):
+            if it < NB:
+                stage_stats(it)
+            if 0 <= it - 1 < NB:
+                stage_main(it - 1)
+            if 0 <= it - 2 < NB:
+                stage_post(it - 2)

@@ -21,8 +21,8 @@ PASSES = 2
 EPS = 1e-5
 FLOPS = 2 * TOKENS * DIM * 256
 
-P2_ENGINE = ("v", "s", "v", "s")
-EXIT_ENGINE = ("s", "s", "s", "s", "s", "s", "s", "s")
+P2_ENGINE = ("g", "g", "g", "g")
+EXIT_ENGINE = ("s", "s", "s", "v", "s", "s", "s", "s")
 OUT_ENGINE = ("s", "s", "s")
 
 
@@ -179,13 +179,9 @@ def tile_gau_pa_t_kernel(
             qkT = post.tile([P, BLOCK], F32, tag="qkT")
             nc.scalar.activation(out=qkT[:], in_=accs[1][:], func=ACT.Silu, bias=cols[:, 17:18], scale=1.0)
             qT = post.tile([P, BLOCK], F32, tag="qT")
-            nc.vector.tensor_scalar(
-                out=qT[:], in0=qkT[:], scalar1=cols[:, 18:19], scalar2=cols[:, 20:21], op0=ALU.mult, op1=ALU.add
-            )
+            nc.scalar.activation(out=qT[:], in_=qkT[:], func=ACT.Identity, scale=cols[:, 18:19], bias=cols[:, 20:21])
             kT = post.tile([P, BLOCK], F32, tag="kT")
-            nc.vector.tensor_scalar(
-                out=kT[:], in0=qkT[:], scalar1=cols[:, 19:20], scalar2=cols[:, 21:22], op0=ALU.mult, op1=ALU.add
-            )
+            nc.scalar.activation(out=kT[:], in_=qkT[:], func=ACT.Identity, scale=cols[:, 19:20], bias=cols[:, 21:22])
             for i, src in enumerate((hidT, qT, kT)):
                 ot = pot.tile([P, BLOCK], F32, tag="ot")
                 for s in range(SUB):

@@ -21,33 +21,25 @@ PASSES = 2
 EPS = 1e-5
 FLOPS = 2 * TOKENS * DIM * 256
 
-P2_ENGINE = ("g", "g", "g", "g")
-EXIT_ENGINE = ("s", "s", "s", "v", "s", "s", "s", "s")
-OUT_ENGINE = ("s", "s", "s")
-
 
 def tile_gau_pa_t_kernel(
     tc, x, ln_scale, ln_bias, W_hidden, b_hidden, W_qk, b_qk, os_weight, os_bias, out_0, out_1, out_2, out_3
 ):
     nc = tc.nc
     xv = x.flatten_outer_dims().rearrange("(b p s) k -> b p s k", p=P, s=SUB)
-    vv = out_0.flatten_outer_dims().rearrange("(b p s) d -> b p s d", p=P, s=SUB)
-    gv = out_1.flatten_outer_dims().rearrange("(b p s) d -> b p s d", p=P, s=SUB)
-    qv = out_2.flatten_outer_dims().rearrange("(b p s) d -> b p s d", p=P, s=SUB)
-    kv = out_3.flatten_outer_dims().rearrange("(b p s) d -> b p s d", p=P, s=SUB)
+    outv = [o.flatten_outer_dims().rearrange("(b p s) d -> b p s d", p=P, s=SUB) for o in (out_0, out_1, out_2, out_3)]
 
-    with tc.tile_pool(name="const", bufs=1) as const, tc.tile_pool(name="xin", bufs=4) as xin, tc.tile_pool(
-        name="stat", bufs=4
-    ) as stat, tc.tile_pool(name="ynorm", bufs=8) as ynorm, tc.tile_pool(name="mid", bufs=2) as mid, tc.tile_pool(
+    with tc.tile_pool(name="const", bufs=1) as const, tc.tile_pool(name="xin", bufs=5) as xin, tc.tile_pool(
+        name="stat", bufs=5
+    ) as stat, tc.tile_pool(name="ynorm", bufs=8) as ynorm, tc.tile_pool(name="mid", bufs=3) as mid, tc.tile_pool(
         name="quant", bufs=4
-    ) as quant, tc.tile_pool(name="post", bufs=2) as post, tc.tile_pool(name="outs", bufs=3) as outs, tc.psum_pool(
+    ) as quant, tc.tile_pool(name="post", bufs=3) as post, tc.tile_pool(name="outs", bufs=3) as outs, tc.psum_pool(
         name="pyt", bufs=4
-    ) as pyt, tc.psum_pool(name="pacc", bufs=2) as pacc, tc.psum_pool(name="pot", bufs=2) as pot:
+    ) as pyt, tc.psum_pool(name="pacc", bufs=2) as pacc, tc.psum_pool(name="pot", bufs=2) as pot, tc.manual_schedule():
         ident = const.tile([P, P], F32)
         make_identity(nc, ident[:])
         neghalf = const.tile([P, SUB], F32)
         nc.gpsimd.memset(neghalf[:], -0.5)
-
         rows = const.tile([P, P], BF16)
         nc.vector.memset(rows[:], 0.0)
         nc.scalar.dma_start(out=rows[0:8, :], in_=ln_scale.rearrange("(c p) -> c p", p=P))
@@ -59,157 +51,220 @@ def tile_gau_pa_t_kernel(
         wraw = const.tile([P, 2, PASSES * PACK, P], BF16)
         nc.scalar.dma_start(out=wraw[:, 0], in_=W_hidden.rearrange("(c p) n -> p c n", p=P))
         nc.scalar.dma_start(out=wraw[:, 1], in_=W_qk.rearrange("(c p) n -> p c n", p=P))
-
         rows32 = const.tile([P, P], F32)
-        nc.vector.tensor_copy(out=rows32[:], in_=rows[:])
-        colps = pot.tile([P, BLOCK], F32, tag="ot")
-        nc.tensor.transpose(out=colps[:, 0:P], in_=rows32[:], identity=ident[:])
         cols = const.tile([P, 32], F32)
-        nc.vector.tensor_copy(out=cols[:], in_=colps[:, 0:32])
-
         wgrp = const.tile([P, 2, PASSES, P, PACK], BF16, align_bytes=64)
-        for w in range(2):
-            nc.vector.tensor_copy(
-                out=wgrp[:, w],
-                in_=wraw[:, w].rearrange("p (g j) n -> p g n j", j=PACK),
-            )
         wcodes = const.tile([P, 2 * PASSES * P], U32, align_bytes=64)
         wscale = const.tile([P, 2 * PASSES * P], U8, align_bytes=64)
-        nc.vector.quantize_mx(
-            out=wcodes[:].bitcast(FP8X4),
-            scales=wscale[:],
-            in_=wgrp[:].rearrange("p w g n j -> p (w g n j)"),
-        )
 
-        state = {}
+        def prepare_constants():
+            nc.vector.tensor_copy(out=rows32[:], in_=rows[:])
+            colps = pot.tile([P, BLOCK], F32, tag="ot", name="colps")
+            nc.tensor.transpose(out=colps[:, 0:P], in_=rows32[:], identity=ident[:])
+            for w in range(2):
+                nc.vector.tensor_copy(out=wgrp[:, w], in_=wraw[:, w].rearrange("p (g j) n -> p g n j", j=PACK))
+            nc.vector.tensor_copy(out=cols[:], in_=colps[:, 0:32])
+            nc.vector.quantize_mx(
+                out=wcodes[:].bitcast(FP8X4), scales=wscale[:], in_=wgrp[:].rearrange("p w g n j -> p (w g n j)")
+            )
 
-        def stage_stats(b):
-            xb = xin.tile([P, SUB, DIM], BF16, tag="xb")
-            nc.sync.dma_start(out=xb[:], in_=xv[b])
-            st = stat.tile([P, SUB, 2, 6], F32, tag="st")
-            mv = stat.tile([P, SUB, 2], F32, tag="mv")
-            for s in range(SUB):
-                for h in range(2):
-                    nc.vector.bn_stats(out=st[:, s, h, :], in_=xb[:, s, 512 * h : 512 * h + 512])
-                nc.vector.bn_aggr(out=mv[:, s, :], in_=st[:, s].rearrange("p h d -> p (h d)"))
-            ve = stat.tile([P, SUB], F32, tag="ve")
+        blocks = [{} for b in range(NB)]
+
+        def live(b):
+            return 0 <= b < NB
+
+        def load(b):
+            if not live(b):
+                return
+            xb = xin.tile([P, SUB, DIM], BF16, tag="xb", name="xb")
+            blocks[b]["xb"] = xb
+            if b == 0:
+                for s in range(SUB):
+                    nc.sync.dma_start(out=xb[:, s, :], in_=xv[b][:, s, :])
+            else:
+                nc.sync.dma_start(out=xb[:], in_=xv[b])
+
+        def stats(b):
+            if not live(b):
+                return
+            blk = blocks[b]
+            xb = blk["xb"]
+            st = stat.tile([P, SUB, 2, 6], F32, tag="st", name="st")
+            mv = stat.tile([P, SUB, 2], F32, tag="mv", name="mv")
+            blk["mv"] = mv
+            for s in range(SUB + 1):
+                if s < SUB:
+                    for h in range(2):
+                        nc.vector.bn_stats(out=st[:, s, h, :], in_=xb[:, s, 512 * h : 512 * h + 512])
+                if s > 0:
+                    nc.vector.bn_aggr(out=mv[:, s - 1, :], in_=st[:, s - 1].rearrange("p h d -> p (h d)"))
+            ve = stat.tile([P, SUB], F32, tag="ve", name="ve")
             nc.gpsimd.tensor_scalar(out=ve[:], in0=mv[:, :, 1], scalar1=EPS, scalar2=1.0, op0=ALU.add, op1=ALU.mult)
-            rstd = stat.tile([P, SUB], F32, tag="rstd")
+            rstd = stat.tile([P, SUB], F32, tag="rstd", name="rstd")
             nc.gpsimd.tensor_tensor(out=rstd[:], in0=ve[:], in1=neghalf[:], op=ALU.pow)
-            negmu = stat.tile([P, SUB], F32, tag="negmu")
+            negmu = stat.tile([P, SUB], F32, tag="negmu", name="negmu")
             nc.gpsimd.tensor_scalar(
                 out=negmu[:], in0=mv[:, :, 0], scalar1=-1.0, scalar2=0.0, op0=ALU.mult, op1=ALU.add
             )
-            nmr = stat.tile([P, SUB], F32, tag="nmr")
+            nmr = stat.tile([P, SUB], F32, tag="nmr", name="nmr")
             nc.gpsimd.tensor_tensor(out=nmr[:], in0=negmu[:], in1=rstd[:], op=ALU.mult)
-            state[b] = {"xb": xb, "mv": mv, "rstd": rstd, "nmr": nmr}
+            blk["rstd"] = rstd
+            blk["nmr"] = nmr
+            blk["y"] = {}
 
-        def stage_main(b):
-            sb = state[b]
-            xb, mv, rstd, nmr = sb["xb"], sb["mv"], sb["rstd"], sb["nmr"]
-            ys = []
-            for s in range(SUB):
-                y = ynorm.tile([P, DIM], F32, tag="y")
-                eng = P2_ENGINE[s]
-                if eng == "v":
-                    nc.vector.tensor_scalar(
-                        out=y[:], in0=xb[:, s, :], scalar1=mv[:, s, 0:1], scalar2=rstd[:, s : s + 1],
-                        op0=ALU.subtract, op1=ALU.mult,
-                    )
-                elif eng == "s":
-                    nc.scalar.activation(
-                        out=y[:], in_=xb[:, s, :], func=ACT.Identity, scale=rstd[:, s : s + 1], bias=nmr[:, s : s + 1]
-                    )
-                else:
-                    nc.gpsimd.tensor_scalar(
-                        out=y[:], in0=xb[:, s, :], scalar1=rstd[:, s : s + 1], scalar2=nmr[:, s : s + 1],
-                        op0=ALU.mult, op1=ALU.add,
-                    )
-                ys.append(y)
-            planes = mid.tile([P, CHUNKS, BLOCK], BF16, tag="planes")
-            codes = []
-            for g in range(PASSES):
-                for j in range(PACK):
-                    c = PACK * g + j
-                    yt = pyt.tile([P, BLOCK], F32, tag="yt")
-                    for s in range(SUB):
-                        nc.tensor.transpose(
-                            out=yt[:, P * s : P * s + P], in_=ys[s][:, P * c : P * c + P], identity=ident[:]
-                        )
-                    if EXIT_ENGINE[c] == "s":
-                        nc.scalar.activation(
-                            out=planes[:, c, :], in_=yt[:], func=ACT.Identity,
-                            scale=cols[:, c : c + 1], bias=cols[:, 8 + c : 9 + c],
-                        )
-                    else:
-                        nc.vector.tensor_scalar(
-                            out=planes[:, c, :], in0=yt[:], scalar1=cols[:, c : c + 1], scalar2=cols[:, 8 + c : 9 + c],
-                            op0=ALU.mult, op1=ALU.add,
-                        )
-                grp = quant.tile([P, BLOCK * PACK], BF16, tag="grp", align_bytes=64)
-                nc.vector.tensor_copy(
-                    out=grp[:].rearrange("p (c i t) -> p c t i", i=4, t=PACK),
-                    in_=planes[:, PACK * g : PACK * g + PACK, :].rearrange("p t (c i) -> p c t i", i=4),
+        def normalise(b, s):
+            if not live(b):
+                return
+            blk = blocks[b]
+            y = ynorm.tile([P, DIM], F32, tag="y", name="y")
+            blk["y"][s] = y
+            if s % 2 == 0:
+                nc.vector.tensor_scalar(
+                    out=y[:], in0=blk["xb"][:, s, :], scalar1=blk["mv"][:, s, 0:1], scalar2=blk["rstd"][:, s : s + 1],
+                    op0=ALU.subtract, op1=ALU.mult,
                 )
-                cd = quant.tile([P, BLOCK], U32, tag="cd", align_bytes=64)
-                sc = quant.tile([P, BLOCK], U8, tag="sc", align_bytes=64)
-                nc.vector.quantize_mx(out=cd[:].bitcast(FP8X4), scales=sc[:], in_=grp[:])
-                codes.append((cd, sc))
-            sb["codes"] = codes
+            else:
+                nc.scalar.activation(
+                    out=y[:], in_=blk["xb"][:, s, :], func=ACT.Identity,
+                    scale=blk["rstd"][:, s : s + 1], bias=blk["nmr"][:, s : s + 1],
+                )
 
-        def stage_post(b):
-            codes = state[b]["codes"]
-            accs = []
+        def turn(b, c):
+            if not live(b):
+                return
+            blk = blocks[b]
+            yt = pyt.tile([P, BLOCK], F32, tag="yt", name="yt")
+            blk["yt%d" % c] = yt
+            for s in range(SUB):
+                nc.tensor.transpose(out=yt[:, P * s : P * s + P], in_=blk["y"][s][:, P * c : P * c + P], identity=ident[:])
+
+        def affine(b, c):
+            if not live(b):
+                return
+            blk = blocks[b]
+            if c == 0:
+                blk["planes"] = mid.tile([P, CHUNKS, BLOCK], BF16, tag="planes", name="planes")
+            nc.scalar.activation(
+                out=blk["planes"][:, c, :], in_=blk["yt%d" % c][:], func=ACT.Identity,
+                scale=cols[:, c : c + 1], bias=cols[:, 8 + c : 9 + c],
+            )
+
+        def regroup(b, g):
+            if not live(b):
+                return
+            blk = blocks[b]
+            grp = quant.tile([P, BLOCK * PACK], BF16, tag="grp", name="grp", align_bytes=64)
+            blk["grp%d" % g] = grp
+            nc.vector.tensor_copy(
+                out=grp[:].rearrange("p (c i t) -> p c t i", i=4, t=PACK),
+                in_=blk["planes"][:, PACK * g : PACK * g + PACK, :].rearrange("p t (c i) -> p c t i", i=4),
+            )
+
+        def quantise(b, g):
+            if not live(b):
+                return
+            blk = blocks[b]
+            cd = quant.tile([P, BLOCK], U32, tag="cd", name="cd", align_bytes=64)
+            sc = quant.tile([P, BLOCK], U8, tag="sc", name="sc", align_bytes=64)
+            nc.vector.quantize_mx(out=cd[:].bitcast(FP8X4), scales=sc[:], in_=blk["grp%d" % g][:])
+            blk["cd%d" % g] = cd
+            blk["sc%d" % g] = sc
+
+        def project(b):
+            if not live(b):
+                return
+            blk = blocks[b]
             for w in range(2):
-                acc = pacc.tile([P, BLOCK], F32, tag="acc")
+                acc = pacc.tile([P, BLOCK], F32, tag="acc", name="acc")
+                blk["acc%d" % w] = acc
                 for g in range(PASSES):
                     o = (w * PASSES + g) * P
                     nc.tensor.matmul_mx(
                         out=acc[:],
                         lhsT=wcodes[:, o : o + P].bitcast(FP8X4),
                         lhsT_scale=wscale[:, o : o + P],
-                        rhs=codes[g][0][:].bitcast(FP8X4),
-                        rhs_scale=codes[g][1][:],
+                        rhs=blk["cd%d" % g][:].bitcast(FP8X4),
+                        rhs_scale=blk["sc%d" % g][:],
                         start=(g == 0),
                         stop=(g == PASSES - 1),
                     )
-                accs.append(acc)
-            hidT = post.tile([P, BLOCK], F32, tag="hidT")
-            nc.scalar.activation(out=hidT[:], in_=accs[0][:], func=ACT.Silu, bias=cols[:, 16:17], scale=1.0)
-            qkT = post.tile([P, BLOCK], F32, tag="qkT")
-            nc.scalar.activation(out=qkT[:], in_=accs[1][:], func=ACT.Silu, bias=cols[:, 17:18], scale=1.0)
-            qT = post.tile([P, BLOCK], F32, tag="qT")
-            nc.scalar.activation(out=qT[:], in_=qkT[:], func=ACT.Identity, scale=cols[:, 18:19], bias=cols[:, 20:21])
-            kT = post.tile([P, BLOCK], F32, tag="kT")
-            nc.scalar.activation(out=kT[:], in_=qkT[:], func=ACT.Identity, scale=cols[:, 19:20], bias=cols[:, 21:22])
-            for i, src in enumerate((hidT, qT, kT)):
-                ot = pot.tile([P, BLOCK], F32, tag="ot")
-                for s in range(SUB):
-                    nc.tensor.transpose(out=ot[:, P * s : P * s + P], in_=src[:, P * s : P * s + P], identity=ident[:])
-                res = outs.tile([P, BLOCK], F32, tag="res%d" % i)
-                if i == 0:
-                    dst = res[:].rearrange("p (h s d) -> p s h d", h=2, s=SUB)
-                    srcv = ot[:].rearrange("p (s h d) -> p s h d", s=SUB, h=2)
-                else:
-                    dst = res[:]
-                    srcv = ot[:]
-                if OUT_ENGINE[i] == "s":
-                    nc.scalar.copy(out=dst, in_=srcv)
-                else:
-                    nc.vector.tensor_copy(out=dst, in_=srcv)
-                if i == 0:
-                    halves = res[:].rearrange("p (h s d) -> p h s d", h=2, s=SUB)
-                    nc.sync.dma_start(out=vv[b], in_=halves[:, 0])
-                    nc.sync.dma_start(out=gv[b], in_=halves[:, 1])
-                elif i == 1:
-                    nc.sync.dma_start(out=qv[b], in_=res[:].rearrange("p (s d) -> p s d", s=SUB))
-                else:
-                    nc.sync.dma_start(out=kv[b], in_=res[:].rearrange("p (s d) -> p s d", s=SUB))
 
-        for it in range(NB + 2):
-            if it < NB:
-                stage_stats(it)
-            if 0 <= it - 1 < NB:
-                stage_main(it - 1)
-            if 0 <= it - 2 < NB:
-                stage_post(it - 2)
+        def silu(b, w):
+            if not live(b):
+                return
+            blk = blocks[b]
+            t = post.tile([P, BLOCK], F32, tag="silu%d" % w, name="silu%d" % w)
+            blk["src%d" % (0 if w == 0 else 3)] = t
+            nc.scalar.activation(out=t[:], in_=blk["acc%d" % w][:], func=ACT.Silu, bias=cols[:, 16 + w : 17 + w], scale=1.0)
+
+        def offset_scale(b, i):
+            if not live(b):
+                return
+            blk = blocks[b]
+            t = post.tile([P, BLOCK], F32, tag="os%d" % i, name="os%d" % i)
+            blk["src%d" % (1 + i)] = t
+            nc.vector.tensor_scalar(
+                out=t[:], in0=blk["src3"][:], scalar1=cols[:, 18 + i : 19 + i], scalar2=cols[:, 20 + i : 21 + i],
+                op0=ALU.mult, op1=ALU.add,
+            )
+
+        def turn_back(b, i):
+            if not live(b):
+                return
+            blk = blocks[b]
+            ot = pot.tile([P, BLOCK], F32, tag="ot", name="ot")
+            blk["ot%d" % i] = ot
+            src = blk["src%d" % i]
+            for s in range(SUB):
+                nc.tensor.transpose(out=ot[:, P * s : P * s + P], in_=src[:, P * s : P * s + P], identity=ident[:])
+
+        def store(b, i):
+            if not live(b):
+                return
+            ot = blocks[b]["ot%d" % i]
+            res = outs.tile([P, BLOCK], F32, tag="res%d" % i, name="res%d" % i)
+            if i == 0:
+                nc.scalar.copy(
+                    out=res[:].rearrange("p (h s d) -> p s h d", h=2, s=SUB),
+                    in_=ot[:].rearrange("p (s h d) -> p s h d", s=SUB, h=2),
+                )
+                halves = res[:].rearrange("p (h s d) -> p h s d", h=2, s=SUB)
+                nc.sync.dma_start(out=outv[0][b], in_=halves[:, 0])
+                nc.sync.dma_start(out=outv[1][b], in_=halves[:, 1])
+            else:
+                nc.scalar.copy(out=res[:], in_=ot[:])
+                nc.sync.dma_start(out=outv[1 + i][b], in_=res[:].rearrange("p (s d) -> p s d", s=SUB))
+
+        load(0)
+        for t in range(-3, NB + 2):
+            load(t + 4)
+            silu(t - 2, 0)
+            silu(t - 2, 1)
+            turn_back(t - 2, 0)
+            for c in range(0, 4):
+                affine(t, c)
+            for c in range(4, 8):
+                turn(t, c)
+            regroup(t - 1, 0)
+            regroup(t - 1, 1)
+            normalise(t + 1, 0)
+            quantise(t - 1, 0)
+            quantise(t - 1, 1)
+            normalise(t + 1, 2)
+            project(t - 1)
+            store(t - 2, 0)
+            normalise(t + 1, 1)
+            normalise(t + 1, 3)
+            offset_scale(t - 2, 0)
+            offset_scale(t - 2, 1)
+            turn_back(t - 2, 1)
+            turn_back(t - 2, 2)
+            for c in range(4, 8):
+                affine(t, c)
+            if t == -2:
+                prepare_constants()
+            stats(t + 3)
+            for c in range(0, 4):
+                turn(t + 1, c)
+            store(t - 2, 1)
+            store(t - 2, 2)

@@ -35,7 +35,7 @@ def tile_gau_pa_t_kernel(
         name="quant", bufs=4
     ) as quant, tc.tile_pool(name="post", bufs=3) as post, tc.tile_pool(name="outs", bufs=3) as outs, tc.psum_pool(
         name="pyt", bufs=4
-    ) as pyt, tc.psum_pool(name="pacc", bufs=2) as pacc, tc.psum_pool(name="pot", bufs=2) as pot, tc.manual_schedule():
+    ) as pyt, tc.psum_pool(name="pacc", bufs=2) as pacc, tc.psum_pool(name="pot", bufs=2) as pot:
         ident = const.tile([P, P], F32)
         make_identity(nc, ident[:])
         neghalf = const.tile([P, SUB], F32)

import concourse.mybir as mybir
from concourse.masks import make_identity

F32 = mybir.dt.float32
BF16 = mybir.dt.bfloat16
U32 = mybir.dt.uint32
U8 = mybir.dt.uint8
FP8X4 = mybir.dt.float8_e4m3fn_x4
ALU = mybir.AluOpType
ACT = mybir.ActivationFunctionType

P = 128
DIM = 1024
TOKENS = 8192
SUB = 4
BLOCK = P * SUB
NB = TOKENS // BLOCK
CHUNKS = DIM // P
PACK = 4
PASSES = 2
EPS = 1e-5
FLOPS = 2 * TOKENS * DIM * 256


def tile_gau_pa_t_kernel(
    tc, x, ln_scale, ln_bias, W_hidden, b_hidden, W_qk, b_qk, os_weight, os_bias, out_0, out_1, out_2, out_3
):
    nc = tc.nc
    xv = x.flatten_outer_dims().rearrange("(b p s) k -> b p s k", p=P, s=SUB)
    outv = [o.flatten_outer_dims().rearrange("(b p s) d -> b p s d", p=P, s=SUB) for o in (out_0, out_1, out_2, out_3)]

    with tc.tile_pool(name="const", bufs=1) as const, tc.tile_pool(name="xin", bufs=5) as xin, tc.tile_pool(
        name="stat", bufs=5
    ) as stat, tc.tile_pool(name="ynorm", bufs=8) as ynorm, tc.tile_pool(name="mid", bufs=3) as mid, tc.tile_pool(
        name="quant", bufs=4
    ) as quant, tc.tile_pool(name="post", bufs=3) as post, tc.tile_pool(name="outs", bufs=3) as outs, tc.psum_pool(
        name="pyt", bufs=4
    ) as pyt, tc.psum_pool(name="pacc", bufs=2) as pacc, tc.psum_pool(name="pot", bufs=2) as pot:
        ident = const.tile([P, P], F32)
        make_identity(nc, ident[:])
        neghalf = const.tile([P, SUB], F32)
        nc.gpsimd.memset(neghalf[:], -0.5)
        rows = const.tile([P, P], BF16)
        nc.vector.memset(rows[:], 0.0)
        nc.scalar.dma_start(out=rows[0:8, :], in_=ln_scale.rearrange("(c p) -> c p", p=P))
        nc.scalar.dma_start(out=rows[8:16, :], in_=ln_bias.rearrange("(c p) -> c p", p=P))
        nc.scalar.dma_start(out=rows[16:17, :], in_=b_hidden.rearrange("(c p) -> c p", p=P))
        nc.scalar.dma_start(out=rows[17:18, :], in_=b_qk.rearrange("(c p) -> c p", p=P))
        nc.scalar.dma_start(out=rows[18:20, :], in_=os_weight)
        nc.scalar.dma_start(out=rows[20:22, :], in_=os_bias)
        wraw = const.tile([P, 2, PASSES * PACK, P], BF16)
        nc.scalar.dma_start(out=wraw[:, 0], in_=W_hidden.rearrange("(c p) n -> p c n", p=P))
        nc.scalar.dma_start(out=wraw[:, 1], in_=W_qk.rearrange("(c p) n -> p c n", p=P))
        rows32 = const.tile([P, P], F32)
        cols = const.tile([P, 32], F32)
        wgrp = const.tile([P, 2, PASSES, P, PACK], BF16, align_bytes=64)
        wcodes = const.tile([P, 2 * PASSES * P], U32, align_bytes=64)
        wscale = const.tile([P, 2 * PASSES * P], U8, align_bytes=64)

        def prepare_constants():
            nc.vector.tensor_copy(out=rows32[:], in_=rows[:])
            colps = pot.tile([P, BLOCK], F32, tag="ot", name="colps")
            nc.tensor.transpose(out=colps[:, 0:P], in_=rows32[:], identity=ident[:])
            for w in range(2):
                nc.vector.tensor_copy(out=wgrp[:, w], in_=wraw[:, w].rearrange("p (g j) n -> p g n j", j=PACK))
            nc.vector.tensor_copy(out=cols[:], in_=colps[:, 0:32])
            nc.vector.quantize_mx(
                out=wcodes[:].bitcast(FP8X4), scales=wscale[:], in_=wgrp[:].rearrange("p w g n j -> p (w g n j)")
            )

        blocks = [{} for b in range(NB)]

        def live(b):
            return 0 <= b < NB

        def load(b):
            if not live(b):
                return
            xb = xin.tile([P, SUB, DIM], BF16, tag="xb", name="xb")
            blocks[b]["xb"] = xb
            if b == 0:
                for s in range(SUB):
                    nc.sync.dma_start(out=xb[:, s, :], in_=xv[b][:, s, :])
            else:
                nc.sync.dma_start(out=xb[:], in_=xv[b])

        def stats(b):
            if not live(b):
                return
            blk = blocks[b]
            xb = blk["xb"]
            st = stat.tile([P, SUB, 2, 6], F32, tag="st", name="st")
            mv = stat.tile([P, SUB, 2], F32, tag="mv", name="mv")
            blk["mv"] = mv
            for s in range(SUB + 1):
                if s < SUB:
                    for h in range(2):
                        nc.vector.bn_stats(out=st[:, s, h, :], in_=xb[:, s, 512 * h : 512 * h + 512])
                if s > 0:
                    nc.vector.bn_aggr(out=mv[:, s - 1, :], in_=st[:, s - 1].rearrange("p h d -> p (h d)"))
            ve = stat.tile([P, SUB], F32, tag="ve", name="ve")
            nc.gpsimd.tensor_scalar(out=ve[:], in0=mv[:, :, 1], scalar1=EPS, scalar2=1.0, op0=ALU.add, op1=ALU.mult)
            rstd = stat.tile([P, SUB], F32, tag="rstd", name="rstd")
            nc.gpsimd.tensor_tensor(out=rstd[:], in0=ve[:], in1=neghalf[:], op=ALU.pow)
            negmu = stat.tile([P, SUB], F32, tag="negmu", name="negmu")
            nc.gpsimd.tensor_scalar(
                out=negmu[:], in0=mv[:, :, 0], scalar1=-1.0, scalar2=0.0, op0=ALU.mult, op1=ALU.add
            )
            nmr = stat.tile([P, SUB], F32, tag="nmr", name="nmr")
            nc.gpsimd.tensor_tensor(out=nmr[:], in0=negmu[:], in1=rstd[:], op=ALU.mult)
            blk["rstd"] = rstd
            blk["nmr"] = nmr
            blk["y"] = {}

        def normalise(b, s):
            if not live(b):
                return
            blk = blocks[b]
            y = ynorm.tile([P, DIM], F32, tag="y", name="y")
            blk["y"][s] = y
            if s % 2 == 0:
                nc.vector.tensor_scalar(
                    out=y[:], in0=blk["xb"][:, s, :], scalar1=blk["mv"][:, s, 0:1], scalar2=blk["rstd"][:, s : s + 1],
                    op0=ALU.subtract, op1=ALU.mult,
                )
            else:
                nc.scalar.activation(
                    out=y[:], in_=blk["xb"][:, s, :], func=ACT.Identity,
                    scale=blk["rstd"][:, s : s + 1], bias=blk["nmr"][:, s : s + 1],
                )

        def turn(b, c):
            if not live(b):
                return
            blk = blocks[b]
            yt = pyt.tile([P, BLOCK], F32, tag="yt", name="yt")
            blk["yt%d" % c] = yt
            for s in range(SUB):
                nc.tensor.transpose(out=yt[:, P * s : P * s + P], in_=blk["y"][s][:, P * c : P * c + P], identity=ident[:])

        def affine(b, c):
            if not live(b):
                return
            blk = blocks[b]
            if c == 0:
                blk["planes"] = mid.tile([P, CHUNKS, BLOCK], BF16, tag="planes", name="planes")
            nc.scalar.activation(
                out=blk["planes"][:, c, :], in_=blk["yt%d" % c][:], func=ACT.Identity,
                scale=cols[:, c : c + 1], bias=cols[:, 8 + c : 9 + c],
            )

        def regroup(b, g):
            if not live(b):
                return
            blk = blocks[b]
            grp = quant.tile([P, BLOCK * PACK], BF16, tag="grp", name="grp", align_bytes=64)
            blk["grp%d" % g] = grp
            nc.vector.tensor_copy(
                out=grp[:].rearrange("p (c i t) -> p c t i", i=4, t=PACK),
                in_=blk["planes"][:, PACK * g : PACK * g + PACK, :].rearrange("p t (c i) -> p c t i", i=4),
            )

        def quantise(b, g):
            if not live(b):
                return
            blk = blocks[b]
            cd = quant.tile([P, BLOCK], U32, tag="cd", name="cd", align_bytes=64)
            sc = quant.tile([P, BLOCK], U8, tag="sc", name="sc", align_bytes=64)
            nc.vector.quantize_mx(out=cd[:].bitcast(FP8X4), scales=sc[:], in_=blk["grp%d" % g][:])
            blk["cd%d" % g] = cd
            blk["sc%d" % g] = sc

        def project(b):
            if not live(b):
                return
            blk = blocks[b]
            for w in range(2):
                acc = pacc.tile([P, BLOCK], F32, tag="acc", name="acc")
                blk["acc%d" % w] = acc
                for g in range(PASSES):
                    o = (w * PASSES + g) * P
                    nc.tensor.matmul_mx(
                        out=acc[:],
                        lhsT=wcodes[:, o : o + P].bitcast(FP8X4),
                        lhsT_scale=wscale[:, o : o + P],
                        rhs=blk["cd%d" % g][:].bitcast(FP8X4),
                        rhs_scale=blk["sc%d" % g][:],
                        start=(g == 0),
                        stop=(g == PASSES - 1),
                    )

        def silu(b, w):
            if not live(b):
                return
            blk = blocks[b]
            t = post.tile([P, BLOCK], F32, tag="silu%d" % w, name="silu%d" % w)
            blk["src%d" % (0 if w == 0 else 3)] = t
            nc.scalar.activation(out=t[:], in_=blk["acc%d" % w][:], func=ACT.Silu, bias=cols[:, 16 + w : 17 + w], scale=1.0)

        def offset_scale(b, i):
            if not live(b):
                return
            blk = blocks[b]
            t = post.tile([P, BLOCK], F32, tag="os%d" % i, name="os%d" % i)
            blk["src%d" % (1 + i)] = t
            nc.vector.tensor_scalar(
                out=t[:], in0=blk["src3"][:], scalar1=cols[:, 18 + i : 19 + i], scalar2=cols[:, 20 + i : 21 + i],
                op0=ALU.mult, op1=ALU.add,
            )

        def turn_back(b, i):
            if not live(b):
                return
            blk = blocks[b]
            ot = pot.tile([P, BLOCK], F32, tag="ot", name="ot")
            blk["ot%d" % i] = ot
            src = blk["src%d" % i]
            for s in range(SUB):
                nc.tensor.transpose(out=ot[:, P * s : P * s + P], in_=src[:, P * s : P * s + P], identity=ident[:])

        def store(b, i):
            if not live(b):
                return
            ot = blocks[b]["ot%d" % i]
            res = outs.tile([P, BLOCK], F32, tag="res%d" % i, name="res%d" % i)
            if i == 0:
                nc.scalar.copy(
                    out=res[:].rearrange("p (h s d) -> p s h d", h=2, s=SUB),
                    in_=ot[:].rearrange("p (s h d) -> p s h d", s=SUB, h=2),
                )
                halves = res[:].rearrange("p (h s d) -> p h s d", h=2, s=SUB)
                nc.sync.dma_start(out=outv[0][b], in_=halves[:, 0])
                nc.sync.dma_start(out=outv[1][b], in_=halves[:, 1])
            else:
                nc.scalar.copy(out=res[:], in_=ot[:])
                nc.sync.dma_start(out=outv[1 + i][b], in_=res[:].rearrange("p (s d) -> p s d", s=SUB))

        load(0)
        for t in range(-3, NB + 2):
            load(t + 4)
            silu(t - 2, 0)
            silu(t - 2, 1)
            turn_back(t - 2, 0)
            for c in range(0, 4):
                affine(t, c)
            for c in range(4, 8):
                turn(t, c)
            regroup(t - 1, 0)
            regroup(t - 1, 1)
            normalise(t + 1, 0)
            quantise(t - 1, 0)
            quantise(t - 1, 1)
            normalise(t + 1, 2)
            project(t - 1)
            store(t - 2, 0)
            normalise(t + 1, 1)
            normalise(t + 1, 3)
            offset_scale(t - 2, 0)
            offset_scale(t - 2, 1)
            turn_back(t - 2, 1)
            turn_back(t - 2, 2)
            for c in range(4, 8):
                affine(t, c)
            if t == -2:
                prepare_constants()
            stats(t + 3)
            for c in range(0, 4):
                turn(t + 1, c)
            store(t - 2, 1)
            store(t - 2, 2)
